import numpy as np
import ml_dtypes


def mxq(x, axis, fmt="e4m3"):
    dtype, down = {"e4m3": (ml_dtypes.float8_e4m3fn, 7), "e5m2": (ml_dtypes.float8_e5m2, 14)}[fmt]
    v = np.moveaxis(np.asarray(x, np.float32).astype(ml_dtypes.bfloat16).astype(np.float64), axis, -1)
    blocks = v.reshape(v.shape[:-1] + (-1, 32))
    amax = np.abs(blocks).max(-1, keepdims=True)
    byte = np.maximum(np.where(amax > 0, np.frexp(amax)[1] - 1 + 127, 0) - down, 1)
    scale = np.exp2(byte - 127.0)
    codes = (blocks / scale).astype(np.float32).astype(dtype).astype(np.float64)
    return np.moveaxis((codes * scale).reshape(v.shape), -1, axis)


WIDE = False


def mx_kscale(k):
    if not WIDE:
        return np.ones(k)
    levels = np.array([10, -10, 5, -5, 0])
    a = np.random.permutation(np.resize(levels, k // 512 * 4)).reshape(k // 512, 4)
    idx = np.arange(k)
    return np.exp2(a[idx // 512, idx % 128 // 32])


BF16 = ml_dtypes.bfloat16


def bf(x):
    return np.asarray(x, np.float32).astype(BF16)


def f64(x):
    return np.asarray(x).astype(np.float64)


B, C, D, T, H, W, P = 4, 256, 512, 8, 16, 16, 2
N = T * H * W
BN_EPS = 1e-5


def setup_inputs():
    s = mx_kscale(D)
    return {"y": bf(np.random.standard_normal((B, D, T, H, W)) * 0.3 * np.sqrt(D) * s[None, :, None, None, None]),
            "w_w": bf(np.random.standard_normal((C, D)) / (0.3 * D) / s[None, :]),
            "w_b": bf(np.random.standard_normal(C) * 0.3),
            "bn_gamma": bf(np.random.standard_normal(C))}


def reference(y, w_w, w_b, bn_gamma):
    wy = (mxq(f64(w_w), 1, "e4m3") @ mxq(f64(y).reshape(B, D, N), 1, "e4m3")) + f64(w_b)[None, :, None]
    wy = wy.reshape(B, C, T, H, W)
    mean = wy.mean(axis=(0, 2, 3, 4))
    var = wy.var(axis=(0, 2, 3, 4))
    return wy, mean, f64(bn_gamma) / np.sqrt(var + BN_EPS)

@@ -1,0 +1,237 @@
+from contextlib import ExitStack
+
+import concourse.mybir as mybir
+from concourse.masks import make_identity
+
+F32 = mybir.dt.float32
+BF16 = mybir.dt.bfloat16
+U32 = mybir.dt.uint32
+U8 = mybir.dt.uint8
+FP8X4 = mybir.dt.float8_e4m3fn_x4
+ACT = mybir.ActivationFunctionType
+ALU = mybir.AluOpType
+
+P = 128
+PACK = 4
+BATCH = 4
+D_IN = P * PACK
+C_OUT = 256
+HALVES = C_OUT // P
+POINTS = 8 * 16 * 16
+CHUNK = 512
+CHUNKS_PER_BATCH = POINTS // CHUNK
+CHUNKS = BATCH * CHUNKS_PER_BATCH
+STORE_CHUNKS = 2
+RUN = 4
+COUNT = BATCH * POINTS
+BN_EPS = 1e-5
+
+FLOPS = 2 * BATCH * C_OUT * D_IN * POINTS
+
+
+def tile_nonlocalblocknd_pc_t_kernel(tc, y, w_w, w_b, bn_gamma, out_0, out_1, out_2):
+    nc = tc.nc
+    with ExitStack() as ctx:
+        const = ctx.enter_context(tc.tile_pool(name="const", bufs=1))
+        y_pool = ctx.enter_context(tc.tile_pool(name="y_in", bufs=1))
+        grouped_pool = ctx.enter_context(tc.tile_pool(name="grouped", bufs=4))
+        mx_pool = ctx.enter_context(tc.tile_pool(name="mx", bufs=4))
+        wy_pool = ctx.enter_context(tc.tile_pool(name="wy", bufs=BATCH * HALVES))
+        squared_pool = ctx.enter_context(tc.tile_pool(name="squared", bufs=4))
+        turn_psum = ctx.enter_context(tc.psum_pool(name="turn", bufs=1))
+        acc_psum = ctx.enter_context(tc.psum_pool(name="acc", bufs=6))
+
+        w_sb = const.tile([P, HALVES * D_IN], BF16, name="w_sb")
+        nc.sync.dma_start(
+            out=w_sb[:].rearrange("o (m d) -> o m d", m=HALVES),
+            in_=w_w.rearrange("(m o) d -> o m d", o=P),
+        )
+        y_rows = y.rearrange("b (p t) f h w -> b p t (f h w)", t=PACK)
+        y_chunk = []
+        for q in range(CHUNKS_PER_BATCH):
+            piece = y_pool.tile([P, PACK, CHUNK], BF16, name="y_first_%d" % q)
+            nc.sync.dma_start(out=piece[:], in_=y_rows[0, :, :, q * CHUNK : (q + 1) * CHUNK])
+            y_chunk.append(piece[:])
+        for b in range(1, BATCH):
+            whole = y_pool.tile([P, PACK, POINTS], BF16, name="y_batch_%d" % b)
+            nc.sync.dma_start(out=whole[:], in_=y_rows[b])
+            for q in range(CHUNKS_PER_BATCH):
+                y_chunk.append(whole[:, :, q * CHUNK : (q + 1) * CHUNK])
+        vec_rows = const.tile([2 * HALVES, P], BF16, name="vec_rows")
+        nc.scalar.dma_start(out=vec_rows[0:HALVES, :], in_=w_b.rearrange("(r c) -> r c", c=P))
+        nc.scalar.dma_start(
+            out=vec_rows[HALVES : 2 * HALVES, :], in_=bn_gamma.rearrange("(r c) -> r c", c=P)
+        )
+
+        ident = const.tile([P, P], F32, name="ident")
+        make_identity(nc, ident[:])
+        one = const.tile([P, 1], F32, name="one")
+        nc.vector.memset(one[:], 1.0)
+        warm = const.tile([P, 1], F32, name="warm")
+        nc.scalar.activation(out=warm[:], in_=one[:], func=ACT.Sqrt)
+        stats = const.tile([P, 3, HALVES, CHUNKS], F32, name="stats")
+        nc.vector.memset(stats[:], 0.0)
+        vec_sq = const.tile([P, P], F32, name="vec_sq")
+        nc.vector.memset(vec_sq[:], 0.0)
+        res_sq = const.tile([P, P], F32, name="res_sq")
+        nc.vector.memset(res_sq[:], 0.0)
+
+        w_words = w_sb[:].bitcast(F32).rearrange("o (m p u) -> o m u p", m=HALVES, u=2)
+        w_turned = turn_psum.tile([P, HALVES, 2, P], F32, name="w_turned")
+        for m in range(HALVES):
+            for u in range(2):
+                nc.tensor.transpose(out=w_turned[:, m, u, :], in_=w_words[:, m, u, :], identity=ident[:])
+        w_grouped = const.tile([P, C_OUT * PACK], BF16, name="w_grouped", align_bytes=64)
+        nc.scalar.copy(
+            out=w_grouped[:].bitcast(F32).rearrange("p (m o u) -> p m o u", m=HALVES, u=2),
+            in_=w_turned[:].rearrange("p m u o -> p m o u"),
+        )
+        w_codes = const.tile([P, C_OUT], U32, name="w_codes", align_bytes=64)
+        w_scales = const.tile([P, C_OUT], U8, name="w_scales", align_bytes=64)
+
+        nc.vector.tensor_copy(out=vec_sq[0 : 2 * HALVES, :], in_=vec_rows[:])
+        vec_turned = turn_psum.tile([P, P], F32, name="vec_turned", tag="small_turn")
+        nc.tensor.transpose(out=vec_turned[:], in_=vec_sq[:], identity=ident[:])
+        per_channel = const.tile([P, 2 * HALVES], F32, name="per_channel")
+        nc.vector.tensor_copy(out=per_channel[:], in_=vec_turned[:, 0 : 2 * HALVES])
+
+        wy_rows = out_0.rearrange("b (m o) f h w -> b m o (f h w)", o=P)
+        grouped_of = {}
+        codes_of = {}
+        scales_of = {}
+        acc_of = {}
+        wy_of = {}
+        neg_shift = const.tile([P, HALVES], F32, name="neg_shift")
+
+        def regroup(j):
+            grouped = grouped_pool.tile([P, CHUNK, PACK], BF16, name="grouped", align_bytes=64)
+            nc.vector.tensor_copy(
+                out=grouped[:].rearrange("p (c i) t -> p c t i", i=RUN),
+                in_=y_chunk[j].rearrange("p t (c i) -> p c t i", i=RUN),
+            )
+            grouped_of[j] = grouped
+
+        def quantise(j):
+            codes = mx_pool.tile([P, CHUNK], U32, name="y_codes", align_bytes=64)
+            scales = mx_pool.tile([P, CHUNK], U8, name="y_scales", align_bytes=64)
+            nc.vector.quantize_mx(
+                out=codes[:].bitcast(FP8X4),
+                scales=scales[:],
+                in_=grouped_of[j][:].rearrange("p n t -> p (n t)"),
+            )
+            codes_of[j] = codes
+            scales_of[j] = scales
+
+        def multiply(j):
+            for m in range(HALVES):
+                acc = acc_psum.tile([P, CHUNK], F32, name="acc")
+                nc.tensor.matmul_mx(
+                    out=acc[:],
+                    lhsT=w_codes[:, m * P : (m + 1) * P].bitcast(FP8X4),
+                    lhsT_scale=w_scales[:, m * P : (m + 1) * P],
+                    rhs=codes_of[j][:].bitcast(FP8X4),
+                    rhs_scale=scales_of[j][:],
+                    start=True,
+                    stop=True,
+                )
+                acc_of[(j, m)] = acc
+
+        def add_bias(j):
+            b = j // CHUNKS_PER_BATCH
+            cols = slice((j % CHUNKS_PER_BATCH) * CHUNK, (j % CHUNKS_PER_BATCH + 1) * CHUNK)
+            for m in range(HALVES):
+                if j % CHUNKS_PER_BATCH == 0:
+                    wy_of[(b, m)] = wy_pool.tile([P, POINTS], F32, name="wy")
+                if m == 1 and j % 2 == 1:
+                    nc.vector.tensor_scalar(
+                        out=wy_of[(b, m)][:, cols],
+                        in0=acc_of[(j, m)][:],
+                        scalar1=per_channel[:, m : m + 1],
+                        scalar2=None,
+                        op0=ALU.add,
+                        op1=ALU.add,
+                        accum_out=stats[:, 1, m, j : j + 1],
+                    )
+                else:
+                    nc.scalar.activation(
+                        out=wy_of[(b, m)][:, cols],
+                        in_=acc_of[(j, m)][:],
+                        func=ACT.Identity,
+                        bias=per_channel[:, m : m + 1],
+                        accum_out=stats[:, 0, m, j : j + 1],
+                    )
+
+        def square(j):
+            b = j // CHUNKS_PER_BATCH
+            cols = slice((j % CHUNKS_PER_BATCH) * CHUNK, (j % CHUNKS_PER_BATCH + 1) * CHUNK)
+            for m in range(HALVES):
+                squared = squared_pool.tile([P, CHUNK], F32, name="squared")
+                nc.scalar.activation(
+                    out=squared[:],
+                    in_=wy_of[(b, m)][:, cols],
+                    func=ACT.Square,
+                    bias=neg_shift[:, m : m + 1],
+                    accum_out=stats[:, 2, m, j : j + 1],
+                )
+
+        def store(j):
+            b = j // CHUNKS_PER_BATCH
+            last = (j % CHUNKS_PER_BATCH + 1) * CHUNK
+            cols = slice(last - STORE_CHUNKS * CHUNK, last)
+            for m in range(HALVES):
+                nc.sync.dma_start(out=wy_rows[b, m, :, cols], in_=wy_of[(b, m)][:, cols])
+
+        for step in range(CHUNKS + 3):
+            if step < CHUNKS:
+                regroup(step)
+            if step == 0:
+                nc.vector.quantize_mx(out=w_codes[:].bitcast(FP8X4), scales=w_scales[:], in_=w_grouped[:])
+            if 1 <= step <= CHUNKS:
+                quantise(step - 1)
+                multiply(step - 1)
+            if 2 <= step <= CHUNKS + 1:
+                add_bias(step - 2)
+                if (step - 2) % STORE_CHUNKS == STORE_CHUNKS - 1:
+                    store(step - 2)
+            if step == 2:
+                nc.vector.tensor_scalar(
+                    out=neg_shift[:], in0=stats[:, 0, :, 0], scalar1=-1.0 / CHUNK, scalar2=None, op0=ALU.mult
+                )
+            if step >= 3:
+                square(step - 3)
+
+        sums = const.tile([P, 2 * HALVES], F32, name="sums")
+        nc.vector.tensor_reduce(
+            out=sums[:],
+            in_=stats[:, 0:2].rearrange("p e m c -> p (e m) c"),
+            axis=mybir.AxisListType.X,
+            op=ALU.add,
+        )
+        total = const.tile([P, HALVES], F32, name="total")
+        nc.vector.tensor_tensor(out=total[:], in0=sums[:, 0:HALVES], in1=sums[:, HALVES : 2 * HALVES], op=ALU.add)
+        nc.vector.tensor_scalar(out=res_sq[:, 0:HALVES], in0=total[:], scalar1=1.0 / COUNT, scalar2=None, op0=ALU.mult)
+        off = const.tile([P, HALVES], F32, name="off")
+        nc.vector.tensor_tensor(out=off[:], in0=res_sq[:, 0:HALVES], in1=neg_shift[:], op=ALU.add)
+        off2 = const.tile([P, HALVES], F32, name="off2")
+        nc.vector.tensor_tensor(out=off2[:], in0=off[:], in1=off[:], op=ALU.mult)
+        squares = const.tile([P, HALVES], F32, name="squares")
+        nc.vector.tensor_reduce(out=squares[:], in_=stats[:, 2], axis=mybir.AxisListType.X, op=ALU.add)
+        var = const.tile([P, HALVES], F32, name="var")
+        nc.vector.scalar_tensor_tensor(
+            out=var[:], in0=squares[:], scalar=1.0 / COUNT, in1=off2[:], op0=ALU.mult, op1=ALU.subtract
+        )
+        var_eps = const.tile([P, HALVES], F32, name="var_eps")
+        nc.vector.tensor_scalar(out=var_eps[:], in0=var[:], scalar1=0.0, scalar2=BN_EPS, op0=ALU.max, op1=ALU.add)
+        std = const.tile([P, HALVES], F32, name="std")
+        nc.scalar.activation(out=std[:], in_=var_eps[:], func=ACT.Sqrt)
+        inv_std = const.tile([P, HALVES], F32, name="inv_std")
+        nc.vector.reciprocal(out=inv_std[:], in_=std[:])
+        nc.vector.tensor_tensor(
+            out=res_sq[:, HALVES : 2 * HALVES], in0=inv_std[:], in1=per_channel[:, HALVES : 2 * HALVES], op=ALU.mult
+        )
+        res_turned = turn_psum.tile([P, P], F32, name="res_turned", tag="small_turn")
+        nc.tensor.transpose(out=res_turned[:], in_=res_sq[:], identity=ident[:])
+        res_rows = const.tile([P, P], F32, name="res_rows")
+        nc.vector.tensor_copy(out=res_rows[:], in_=res_turned[:])
+        nc.sync.dma_start(out=out_1.rearrange("(r c) -> r c", c=P), in_=res_rows[0:HALVES, :])
+        nc.sync.dma_start(out=out_2.rearrange("(r c) -> r c", c=P), in_=res_rows[HALVES : 2 * HALVES, :])

@@ -22,6 +22,7 @@ CHUNK = 512
 CHUNKS_PER_BATCH = POINTS // CHUNK
 CHUNKS = BATCH * CHUNKS_PER_BATCH
 STORE_CHUNKS = 2
+VECTOR_FROM = 10
 RUN = 4
 COUNT = BATCH * POINTS
 BN_EPS = 1e-5
@@ -35,11 +36,12 @@ def tile_nonlocalblocknd_pc_t_kernel(tc, y, w_w, w_b, bn_gamma, out_0, out_1, ou
         const = ctx.enter_context(tc.tile_pool(name="const", bufs=1))
         y_pool = ctx.enter_context(tc.tile_pool(name="y_in", bufs=1))
         grouped_pool = ctx.enter_context(tc.tile_pool(name="grouped", bufs=4))
-        mx_pool = ctx.enter_context(tc.tile_pool(name="mx", bufs=4))
+        mx_pool = ctx.enter_context(tc.tile_pool(name="mx", bufs=CHUNKS))
         wy_pool = ctx.enter_context(tc.tile_pool(name="wy", bufs=BATCH * HALVES))
         squared_pool = ctx.enter_context(tc.tile_pool(name="squared", bufs=4))
         turn_psum = ctx.enter_context(tc.psum_pool(name="turn", bufs=1))
         acc_psum = ctx.enter_context(tc.psum_pool(name="acc", bufs=6))
+        ctx.enter_context(tc.manual_schedule())
 
         w_sb = const.tile([P, HALVES * D_IN], BF16, name="w_sb")
         nc.sync.dma_start(
@@ -48,15 +50,14 @@ def tile_nonlocalblocknd_pc_t_kernel(tc, y, w_w, w_b, bn_gamma, out_0, out_1, ou
         )
         y_rows = y.rearrange("b (p t) f h w -> b p t (f h w)", t=PACK)
         y_chunk = []
-        for q in range(CHUNKS_PER_BATCH):
-            piece = y_pool.tile([P, PACK, CHUNK], BF16, name="y_first_%d" % q)
-            nc.sync.dma_start(out=piece[:], in_=y_rows[0, :, :, q * CHUNK : (q + 1) * CHUNK])
-            y_chunk.append(piece[:])
-        for b in range(1, BATCH):
-            whole = y_pool.tile([P, PACK, POINTS], BF16, name="y_batch_%d" % b)
-            nc.sync.dma_start(out=whole[:], in_=y_rows[b])
-            for q in range(CHUNKS_PER_BATCH):
-                y_chunk.append(whole[:, :, q * CHUNK : (q + 1) * CHUNK])
+        for b in range(BATCH):
+            pieces = max(1, CHUNKS_PER_BATCH >> b)
+            width = POINTS // pieces
+            for q in range(pieces):
+                piece = y_pool.tile([P, PACK, width], BF16, name="y_%d_%d" % (b, q))
+                nc.sync.dma_start(out=piece[:], in_=y_rows[b, :, :, q * width : (q + 1) * width])
+                for c in range(0, width, CHUNK):
+                    y_chunk.append(piece[:, :, c : c + CHUNK])
         vec_rows = const.tile([2 * HALVES, P], BF16, name="vec_rows")
         nc.scalar.dma_start(out=vec_rows[0:HALVES, :], in_=w_b.rearrange("(r c) -> r c", c=P))
         nc.scalar.dma_start(
@@ -89,11 +90,11 @@ def tile_nonlocalblocknd_pc_t_kernel(tc, y, w_w, w_b, bn_gamma, out_0, out_1, ou
         w_codes = const.tile([P, C_OUT], U32, name="w_codes", align_bytes=64)
         w_scales = const.tile([P, C_OUT], U8, name="w_scales", align_bytes=64)
 
-        nc.vector.tensor_copy(out=vec_sq[0 : 2 * HALVES, :], in_=vec_rows[:])
+        nc.scalar.copy(out=vec_sq[0 : 2 * HALVES, :], in_=vec_rows[:])
         vec_turned = turn_psum.tile([P, P], F32, name="vec_turned", tag="small_turn")
         nc.tensor.transpose(out=vec_turned[:], in_=vec_sq[:], identity=ident[:])
         per_channel = const.tile([P, 2 * HALVES], F32, name="per_channel")
-        nc.vector.tensor_copy(out=per_channel[:], in_=vec_turned[:, 0 : 2 * HALVES])
+        nc.scalar.copy(out=per_channel[:], in_=vec_turned[:, 0 : 2 * HALVES])
 
         wy_rows = out_0.rearrange("b (m o) f h w -> b m o (f h w)", o=P)
         grouped_of = {}
@@ -142,7 +143,7 @@ def tile_nonlocalblocknd_pc_t_kernel(tc, y, w_w, w_b, bn_gamma, out_0, out_1, ou
             for m in range(HALVES):
                 if j % CHUNKS_PER_BATCH == 0:
                     wy_of[(b, m)] = wy_pool.tile([P, POINTS], F32, name="wy")
-                if m == 1 and j % 2 == 1:
+                if j >= VECTOR_FROM:
                     nc.vector.tensor_scalar(
                         out=wy_of[(b, m)][:, cols],
                         in0=acc_of[(j, m)][:],
@@ -181,24 +182,23 @@ def tile_nonlocalblocknd_pc_t_kernel(tc, y, w_w, w_b, bn_gamma, out_0, out_1, ou
             for m in range(HALVES):
                 nc.sync.dma_start(out=wy_rows[b, m, :, cols], in_=wy_of[(b, m)][:, cols])
 
-        for step in range(CHUNKS + 3):
-            if step < CHUNKS:
-                regroup(step)
-            if step == 0:
-                nc.vector.quantize_mx(out=w_codes[:].bitcast(FP8X4), scales=w_scales[:], in_=w_grouped[:])
-            if 1 <= step <= CHUNKS:
-                quantise(step - 1)
-                multiply(step - 1)
-            if 2 <= step <= CHUNKS + 1:
-                add_bias(step - 2)
-                if (step - 2) % STORE_CHUNKS == STORE_CHUNKS - 1:
-                    store(step - 2)
-            if step == 2:
-                nc.vector.tensor_scalar(
-                    out=neg_shift[:], in0=stats[:, 0, :, 0], scalar1=-1.0 / CHUNK, scalar2=None, op0=ALU.mult
-                )
-            if step >= 3:
-                square(step - 3)
+        regroup(0)
+        nc.vector.quantize_mx(out=w_codes[:].bitcast(FP8X4), scales=w_scales[:], in_=w_grouped[:])
+        quantise(0)
+        regroup(1)
+        for j in range(1, CHUNKS):
+            if j + 1 < CHUNKS:
+                regroup(j + 1)
+            quantise(j)
+
+        for j in range(CHUNKS):
+            multiply(j)
+            add_bias(j)
+            if j == 0:
+                nc.scalar.mul(out=neg_shift[:], in_=stats[:, 0, :, 0], mul=-1.0 / CHUNK)
+            square(j)
+            if j % STORE_CHUNKS == STORE_CHUNKS - 1:
+                store(j)
 
         sums = const.tile([P, 2 * HALVES], F32, name="sums")
         nc.vector.tensor_reduce(

@@ -22,7 +22,7 @@ CHUNK = 512
 CHUNKS_PER_BATCH = POINTS // CHUNK
 CHUNKS = BATCH * CHUNKS_PER_BATCH
 STORE_CHUNKS = 2
-VECTOR_FROM = 10
+VECTOR_FROM = 11
 RUN = 4
 COUNT = BATCH * POINTS
 BN_EPS = 1e-5

@@ -18,27 +18,51 @@ D_IN = P * PACK
 C_OUT = 256
 HALVES = C_OUT // P
 POINTS = 8 * 16 * 16
-CHUNK = 512
-CHUNKS_PER_BATCH = POINTS // CHUNK
-CHUNKS = BATCH * CHUNKS_PER_BATCH
-STORE_CHUNKS = 2
-VECTOR_FROM = 11
+BANK = 512
 RUN = 4
 COUNT = BATCH * POINTS
 BN_EPS = 1e-5
+BLOCK = 32
+
+LOAD_WIDTHS = ((512, 512, 512, 512), (1024, 1024), (2048,), (2048,))
+UNIT_WIDTHS = ((512,) * 4,) * 4
+SQUARE_WIDTHS = ((512, 512, 1024), (2048,), (1536, 512), (512,) * 4)
+STORE_WIDTHS = ((1024, 1024),) * 4
+VECTOR_BANKS = 10
 
 FLOPS = 2 * BATCH * C_OUT * D_IN * POINTS
 
 
+def cut(widths_by_batch):
+    pieces = []
+    for b in range(BATCH):
+        first = 0
+        for width in widths_by_batch[b]:
+            pieces.append((b, first, width))
+            first += width
+        assert first == POINTS
+    return pieces
+
+
 def tile_nonlocalblocknd_pc_t_kernel(tc, y, w_w, w_b, bn_gamma, out_0, out_1, out_2):
     nc = tc.nc
+    loads = cut(LOAD_WIDTHS)
+    units = cut(UNIT_WIDTHS)
+    squares = cut(SQUARE_WIDTHS)
+    stores = cut(STORE_WIDTHS)
+    passes = []
+    for u, (b, first, width) in enumerate(units):
+        for c in range(0, width, BANK):
+            passes.append((u, b, first + c, min(BANK, width), c))
+    slots = max(len(passes), len(squares))
+
     with ExitStack() as ctx:
         const = ctx.enter_context(tc.tile_pool(name="const", bufs=1))
         y_pool = ctx.enter_context(tc.tile_pool(name="y_in", bufs=1))
-        grouped_pool = ctx.enter_context(tc.tile_pool(name="grouped", bufs=4))
-        mx_pool = ctx.enter_context(tc.tile_pool(name="mx", bufs=CHUNKS))
+        grouped_pool = ctx.enter_context(tc.tile_pool(name="grouped", bufs=3))
+        mx_pool = ctx.enter_context(tc.tile_pool(name="mx", bufs=1))
         wy_pool = ctx.enter_context(tc.tile_pool(name="wy", bufs=BATCH * HALVES))
-        squared_pool = ctx.enter_context(tc.tile_pool(name="squared", bufs=4))
+        squared_pool = ctx.enter_context(tc.tile_pool(name="squared", bufs=2))
         turn_psum = ctx.enter_context(tc.psum_pool(name="turn", bufs=1))
         acc_psum = ctx.enter_context(tc.psum_pool(name="acc", bufs=6))
         ctx.enter_context(tc.manual_schedule())
@@ -49,15 +73,18 @@ def tile_nonlocalblocknd_pc_t_kernel(tc, y, w_w, w_b, bn_gamma, out_0, out_1, ou
             in_=w_w.rearrange("(m o) d -> o m d", o=P),
         )
         y_rows = y.rearrange("b (p t) f h w -> b p t (f h w)", t=PACK)
-        y_chunk = []
-        for b in range(BATCH):
-            pieces = max(1, CHUNKS_PER_BATCH >> b)
-            width = POINTS // pieces
-            for q in range(pieces):
-                piece = y_pool.tile([P, PACK, width], BF16, name="y_%d_%d" % (b, q))
-                nc.sync.dma_start(out=piece[:], in_=y_rows[b, :, :, q * width : (q + 1) * width])
-                for c in range(0, width, CHUNK):
-                    y_chunk.append(piece[:, :, c : c + CHUNK])
+        y_piece = {}
+        for b, first, width in loads:
+            piece = y_pool.tile([P, PACK, width], BF16, name="y_%d_%d" % (b, first))
+            nc.sync.dma_start(out=piece[:], in_=y_rows[b, :, :, first : first + width])
+            y_piece[(b, first)] = piece
+
+        def y_view(b, first, width):
+            for lb, lfirst, lwidth in loads:
+                if lb == b and lfirst <= first and first + width <= lfirst + lwidth:
+                    return y_piece[(lb, lfirst)][:, :, first - lfirst : first - lfirst + width]
+            raise ValueError("a unit must lie inside one load")
+
         vec_rows = const.tile([2 * HALVES, P], BF16, name="vec_rows")
         nc.scalar.dma_start(out=vec_rows[0:HALVES, :], in_=w_b.rearrange("(r c) -> r c", c=P))
         nc.scalar.dma_start(
@@ -69,13 +96,13 @@ def tile_nonlocalblocknd_pc_t_kernel(tc, y, w_w, w_b, bn_gamma, out_0, out_1, ou
         one = const.tile([P, 1], F32, name="one")
         nc.vector.memset(one[:], 1.0)
         warm = const.tile([P, 1], F32, name="warm")
-        nc.scalar.activation(out=warm[:], in_=one[:], func=ACT.Sqrt)
-        stats = const.tile([P, 3, HALVES, CHUNKS], F32, name="stats")
+        nc.scalar.activation(out=warm[:], in_=one[:], func=ACT.Abs_reciprocal_sqrt)
+        stats = const.tile([P, 2, HALVES, slots], F32, name="stats")
         nc.vector.memset(stats[:], 0.0)
         vec_sq = const.tile([P, P], F32, name="vec_sq")
         nc.vector.memset(vec_sq[:], 0.0)
-        res_sq = const.tile([P, P], F32, name="res_sq")
-        nc.vector.memset(res_sq[:], 0.0)
+        res_cols = const.tile([P, BLOCK], F32, name="res_cols", align_bytes=64)
+        nc.vector.memset(res_cols[:], 0.0)
 
         w_words = w_sb[:].bitcast(F32).rearrange("o (m p u) -> o m u p", m=HALVES, u=2)
         w_turned = turn_psum.tile([P, HALVES, 2, P], F32, name="w_turned")
@@ -91,7 +118,7 @@ def tile_nonlocalblocknd_pc_t_kernel(tc, y, w_w, w_b, bn_gamma, out_0, out_1, ou
         w_scales = const.tile([P, C_OUT], U8, name="w_scales", align_bytes=64)
 
         nc.scalar.copy(out=vec_sq[0 : 2 * HALVES, :], in_=vec_rows[:])
-        vec_turned = turn_psum.tile([P, P], F32, name="vec_turned", tag="small_turn")
+        vec_turned = turn_psum.tile([P, P], F32, name="vec_turned")
         nc.tensor.transpose(out=vec_turned[:], in_=vec_sq[:], identity=ident[:])
         per_channel = const.tile([P, 2 * HALVES], F32, name="per_channel")
         nc.scalar.copy(out=per_channel[:], in_=vec_turned[:, 0 : 2 * HALVES])
@@ -104,134 +131,134 @@ def tile_nonlocalblocknd_pc_t_kernel(tc, y, w_w, w_b, bn_gamma, out_0, out_1, ou
         wy_of = {}
         neg_shift = const.tile([P, HALVES], F32, name="neg_shift")
 
-        def regroup(j):
-            grouped = grouped_pool.tile([P, CHUNK, PACK], BF16, name="grouped", align_bytes=64)
+        def regroup(u):
+            b, first, width = units[u]
+            grouped = grouped_pool.tile([P, width, PACK], BF16, name="grouped", align_bytes=64)
             nc.vector.tensor_copy(
                 out=grouped[:].rearrange("p (c i) t -> p c t i", i=RUN),
-                in_=y_chunk[j].rearrange("p t (c i) -> p c t i", i=RUN),
+                in_=y_view(b, first, width).rearrange("p t (c i) -> p c t i", i=RUN),
             )
-            grouped_of[j] = grouped
+            grouped_of[u] = grouped
 
-        def quantise(j):
-            codes = mx_pool.tile([P, CHUNK], U32, name="y_codes", align_bytes=64)
-            scales = mx_pool.tile([P, CHUNK], U8, name="y_scales", align_bytes=64)
+        def quantise(u):
+            width = units[u][2]
+            codes = mx_pool.tile([P, width], U32, name="y_codes_%d" % u, align_bytes=64)
+            scales = mx_pool.tile([P, width], U8, name="y_scales_%d" % u, align_bytes=64)
             nc.vector.quantize_mx(
                 out=codes[:].bitcast(FP8X4),
                 scales=scales[:],
-                in_=grouped_of[j][:].rearrange("p n t -> p (n t)"),
+                in_=grouped_of[u][:].rearrange("p n t -> p (n t)"),
             )
-            codes_of[j] = codes
-            scales_of[j] = scales
+            codes_of[u] = codes
+            scales_of[u] = scales
 
-        def multiply(j):
+        def multiply(i):
+            u, b, first, width, c = passes[i]
             for m in range(HALVES):
-                acc = acc_psum.tile([P, CHUNK], F32, name="acc")
+                acc = acc_psum.tile([P, width], F32, name="acc")
                 nc.tensor.matmul_mx(
                     out=acc[:],
                     lhsT=w_codes[:, m * P : (m + 1) * P].bitcast(FP8X4),
                     lhsT_scale=w_scales[:, m * P : (m + 1) * P],
-                    rhs=codes_of[j][:].bitcast(FP8X4),
-                    rhs_scale=scales_of[j][:],
+                    rhs=codes_of[u][:, c : c + width].bitcast(FP8X4),
+                    rhs_scale=scales_of[u][:, c : c + width],
                     start=True,
                     stop=True,
                 )
-                acc_of[(j, m)] = acc
+                acc_of[(i, m)] = acc
 
-        def add_bias(j):
-            b = j // CHUNKS_PER_BATCH
-            cols = slice((j % CHUNKS_PER_BATCH) * CHUNK, (j % CHUNKS_PER_BATCH + 1) * CHUNK)
-            for m in range(HALVES):
-                if j % CHUNKS_PER_BATCH == 0:
-                    wy_of[(b, m)] = wy_pool.tile([P, POINTS], F32, name="wy")
-                if j >= VECTOR_FROM:
-                    nc.vector.tensor_scalar(
-                        out=wy_of[(b, m)][:, cols],
-                        in0=acc_of[(j, m)][:],
-                        scalar1=per_channel[:, m : m + 1],
-                        scalar2=None,
-                        op0=ALU.add,
-                        op1=ALU.add,
-                        accum_out=stats[:, 1, m, j : j + 1],
-                    )
-                else:
-                    nc.scalar.activation(
-                        out=wy_of[(b, m)][:, cols],
-                        in_=acc_of[(j, m)][:],
-                        func=ACT.Identity,
-                        bias=per_channel[:, m : m + 1],
-                        accum_out=stats[:, 0, m, j : j + 1],
-                    )
-
-        def square(j):
-            b = j // CHUNKS_PER_BATCH
-            cols = slice((j % CHUNKS_PER_BATCH) * CHUNK, (j % CHUNKS_PER_BATCH + 1) * CHUNK)
-            for m in range(HALVES):
-                squared = squared_pool.tile([P, CHUNK], F32, name="squared")
+        def add_bias(i, m):
+            u, b, first, width, c = passes[i]
+            if first == 0:
+                wy_of[(b, m)] = wy_pool.tile([P, POINTS], F32, name="wy")
+            if HALVES * i + m >= HALVES * len(passes) - VECTOR_BANKS:
+                nc.vector.tensor_scalar(
+                    out=wy_of[(b, m)][:, first : first + width],
+                    in0=acc_of[(i, m)][:],
+                    scalar1=per_channel[:, m : m + 1],
+                    scalar2=None,
+                    op0=ALU.add,
+                    op1=ALU.add,
+                    accum_out=stats[:, 0, m, i : i + 1],
+                )
+            else:
                 nc.scalar.activation(
-                    out=squared[:],
-                    in_=wy_of[(b, m)][:, cols],
-                    func=ACT.Square,
-                    bias=neg_shift[:, m : m + 1],
-                    accum_out=stats[:, 2, m, j : j + 1],
+                    out=wy_of[(b, m)][:, first : first + width],
+                    in_=acc_of[(i, m)][:],
+                    func=ACT.Identity,
+                    bias=per_channel[:, m : m + 1],
+                    accum_out=stats[:, 0, m, i : i + 1],
                 )
 
-        def store(j):
-            b = j // CHUNKS_PER_BATCH
-            last = (j % CHUNKS_PER_BATCH + 1) * CHUNK
-            cols = slice(last - STORE_CHUNKS * CHUNK, last)
-            for m in range(HALVES):
-                nc.sync.dma_start(out=wy_rows[b, m, :, cols], in_=wy_of[(b, m)][:, cols])
+        def square(g, m):
+            b, first, width = squares[g]
+            squared = squared_pool.tile([P, width], BF16, name="squared")
+            nc.scalar.activation(
+                out=squared[:],
+                in_=wy_of[(b, m)][:, first : first + width],
+                func=ACT.Square,
+                bias=neg_shift[:, m : m + 1],
+                accum_out=stats[:, 1, m, g : g + 1],
+            )
 
         regroup(0)
         nc.vector.quantize_mx(out=w_codes[:].bitcast(FP8X4), scales=w_scales[:], in_=w_grouped[:])
         quantise(0)
         regroup(1)
-        for j in range(1, CHUNKS):
-            if j + 1 < CHUNKS:
-                regroup(j + 1)
-            quantise(j)
+        for u in range(1, len(units)):
+            if u + 1 < len(units):
+                regroup(u + 1)
+            quantise(u)
 
-        for j in range(CHUNKS):
-            multiply(j)
-            add_bias(j)
-            if j == 0:
-                nc.scalar.mul(out=neg_shift[:], in_=stats[:, 0, :, 0], mul=-1.0 / CHUNK)
-            square(j)
-            if j % STORE_CHUNKS == STORE_CHUNKS - 1:
-                store(j)
+        for i, (u, b, first, width, c) in enumerate(passes):
+            done = first + width
+            multiply(i)
+            for m in range(HALVES):
+                add_bias(i, m)
+            if i == 0:
+                nc.scalar.mul(out=neg_shift[:], in_=stats[:, 0, :, 0], mul=-1.0 / width)
+            for g, (gb, gfirst, gwidth) in enumerate(squares):
+                if gb == b and gfirst + gwidth == done:
+                    for m in range(HALVES):
+                        square(g, m)
+            for sb, sfirst, swidth in stores:
+                if sb == b and sfirst + swidth == done:
+                    for m in range(HALVES):
+                        nc.sync.dma_start(
+                            out=wy_rows[b, m, :, sfirst:done], in_=wy_of[(b, m)][:, sfirst:done]
+                        )
 
-        sums = const.tile([P, 2 * HALVES], F32, name="sums")
+        totals = const.tile([P, 2 * HALVES], F32, name="totals")
         nc.vector.tensor_reduce(
-            out=sums[:],
-            in_=stats[:, 0:2].rearrange("p e m c -> p (e m) c"),
-            axis=mybir.AxisListType.X,
-            op=ALU.add,
+            out=totals[:], in_=stats[:].rearrange("p k m c -> p (k m) c"), axis=mybir.AxisListType.X, op=ALU.add
         )
-        total = const.tile([P, HALVES], F32, name="total")
-        nc.vector.tensor_tensor(out=total[:], in0=sums[:, 0:HALVES], in1=sums[:, HALVES : 2 * HALVES], op=ALU.add)
-        nc.vector.tensor_scalar(out=res_sq[:, 0:HALVES], in0=total[:], scalar1=1.0 / COUNT, scalar2=None, op0=ALU.mult)
         off = const.tile([P, HALVES], F32, name="off")
-        nc.vector.tensor_tensor(out=off[:], in0=res_sq[:, 0:HALVES], in1=neg_shift[:], op=ALU.add)
+        nc.vector.scalar_tensor_tensor(
+            out=off[:], in0=totals[:, 0:HALVES], scalar=1.0 / COUNT, in1=neg_shift[:], op0=ALU.mult, op1=ALU.add
+        )
         off2 = const.tile([P, HALVES], F32, name="off2")
         nc.vector.tensor_tensor(out=off2[:], in0=off[:], in1=off[:], op=ALU.mult)
-        squares = const.tile([P, HALVES], F32, name="squares")
-        nc.vector.tensor_reduce(out=squares[:], in_=stats[:, 2], axis=mybir.AxisListType.X, op=ALU.add)
         var = const.tile([P, HALVES], F32, name="var")
         nc.vector.scalar_tensor_tensor(
-            out=var[:], in0=squares[:], scalar=1.0 / COUNT, in1=off2[:], op0=ALU.mult, op1=ALU.subtract
+            out=var[:],
+            in0=totals[:, HALVES : 2 * HALVES],
+            scalar=1.0 / COUNT,
+            in1=off2[:],
+            op0=ALU.mult,
+            op1=ALU.subtract,
         )
-        var_eps = const.tile([P, HALVES], F32, name="var_eps")
-        nc.vector.tensor_scalar(out=var_eps[:], in0=var[:], scalar1=0.0, scalar2=BN_EPS, op0=ALU.max, op1=ALU.add)
-        std = const.tile([P, HALVES], F32, name="std")
-        nc.scalar.activation(out=std[:], in_=var_eps[:], func=ACT.Sqrt)
         inv_std = const.tile([P, HALVES], F32, name="inv_std")
-        nc.vector.reciprocal(out=inv_std[:], in_=std[:])
-        nc.vector.tensor_tensor(
-            out=res_sq[:, HALVES : 2 * HALVES], in0=inv_std[:], in1=per_channel[:, HALVES : 2 * HALVES], op=ALU.mult
+        nc.scalar.activation(out=inv_std[:], in_=var[:], func=ACT.Abs_reciprocal_sqrt, bias=BN_EPS)
+        nc.vector.tensor_scalar(
+            out=res_cols[:, 0:HALVES], in0=totals[:, 0:HALVES], scalar1=1.0 / COUNT, scalar2=None, op0=ALU.mult
         )
-        res_turned = turn_psum.tile([P, P], F32, name="res_turned", tag="small_turn")
-        nc.tensor.transpose(out=res_turned[:], in_=res_sq[:], identity=ident[:])
-        res_rows = const.tile([P, P], F32, name="res_rows")
-        nc.vector.tensor_copy(out=res_rows[:], in_=res_turned[:])
-        nc.sync.dma_start(out=out_1.rearrange("(r c) -> r c", c=P), in_=res_rows[0:HALVES, :])
-        nc.sync.dma_start(out=out_2.rearrange("(r c) -> r c", c=P), in_=res_rows[HALVES : 2 * HALVES, :])
+        nc.vector.tensor_tensor(
+            out=res_cols[:, HALVES : 2 * HALVES], in0=inv_std[:], in1=per_channel[:, HALVES : 2 * HALVES], op=ALU.mult
+        )
+        res_blocks = const.tile([P, BLOCK], F32, name="res_blocks", align_bytes=64)
+        nc.vector.transpose(out=res_blocks[:], in_=res_cols[:])
+        mean_rows = out_1.rearrange("(m q i) -> m q i", m=HALVES, i=BLOCK)
+        gain_rows = out_2.rearrange("(m q i) -> m q i", m=HALVES, i=BLOCK)
+        for m in range(HALVES):
+            nc.sync.dma_start(out=gain_rows[m], in_=res_blocks[HALVES + m : P : BLOCK, :])
+            nc.scalar.dma_start(out=mean_rows[m], in_=res_blocks[m:P:BLOCK, :])

@@ -228,30 +228,30 @@ def tile_nonlocalblocknd_pc_t_kernel(tc, y, w_w, w_b, bn_gamma, out_0, out_1, ou
                             out=wy_rows[b, m, :, sfirst:done], in_=wy_of[(b, m)][:, sfirst:done]
                         )
 
-        totals = const.tile([P, 2 * HALVES], F32, name="totals")
-        nc.vector.tensor_reduce(
-            out=totals[:], in_=stats[:].rearrange("p k m c -> p (k m) c"), axis=mybir.AxisListType.X, op=ALU.add
-        )
+        sums = const.tile([P, HALVES], F32, name="sums")
+        nc.vector.tensor_reduce(out=sums[:], in_=stats[:, 0], axis=mybir.AxisListType.X, op=ALU.add)
         off = const.tile([P, HALVES], F32, name="off")
         nc.vector.scalar_tensor_tensor(
-            out=off[:], in0=totals[:, 0:HALVES], scalar=1.0 / COUNT, in1=neg_shift[:], op0=ALU.mult, op1=ALU.add
+            out=off[:], in0=sums[:], scalar=1.0 / COUNT, in1=neg_shift[:], op0=ALU.mult, op1=ALU.add
         )
         off2 = const.tile([P, HALVES], F32, name="off2")
         nc.vector.tensor_tensor(out=off2[:], in0=off[:], in1=off[:], op=ALU.mult)
+        nc.vector.tensor_scalar(
+            out=res_cols[:, 0:HALVES], in0=sums[:], scalar1=1.0 / COUNT, scalar2=None, op0=ALU.mult
+        )
+        last = len(squares) - 1
+        early = const.tile([P, HALVES], F32, name="early")
+        nc.vector.tensor_reduce(out=early[:], in_=stats[:, 1, :, 0:last], axis=mybir.AxisListType.X, op=ALU.add)
+        rest = const.tile([P, HALVES], F32, name="rest")
+        nc.vector.scalar_tensor_tensor(
+            out=rest[:], in0=early[:], scalar=1.0 / COUNT, in1=off2[:], op0=ALU.mult, op1=ALU.subtract
+        )
         var = const.tile([P, HALVES], F32, name="var")
         nc.vector.scalar_tensor_tensor(
-            out=var[:],
-            in0=totals[:, HALVES : 2 * HALVES],
-            scalar=1.0 / COUNT,
-            in1=off2[:],
-            op0=ALU.mult,
-            op1=ALU.subtract,
+            out=var[:], in0=stats[:, 1, :, last], scalar=1.0 / COUNT, in1=rest[:], op0=ALU.mult, op1=ALU.add
         )
         inv_std = const.tile([P, HALVES], F32, name="inv_std")
         nc.scalar.activation(out=inv_std[:], in_=var[:], func=ACT.Abs_reciprocal_sqrt, bias=BN_EPS)
-        nc.vector.tensor_scalar(
-            out=res_cols[:, 0:HALVES], in0=totals[:, 0:HALVES], scalar1=1.0 / COUNT, scalar2=None, op0=ALU.mult
-        )
         nc.vector.tensor_tensor(
             out=res_cols[:, HALVES : 2 * HALVES], in0=inv_std[:], in1=per_channel[:, HALVES : 2 * HALVES], op=ALU.mult
         )

@@ -101,8 +101,10 @@ def tile_nonlocalblocknd_pc_t_kernel(tc, y, w_w, w_b, bn_gamma, out_0, out_1, ou
         nc.vector.memset(stats[:], 0.0)
         vec_sq = const.tile([P, P], F32, name="vec_sq")
         nc.vector.memset(vec_sq[:], 0.0)
-        res_cols = const.tile([P, BLOCK], F32, name="res_cols", align_bytes=64)
-        nc.vector.memset(res_cols[:], 0.0)
+        mean_cols = const.tile([P, BLOCK], F32, name="mean_cols", align_bytes=64)
+        nc.vector.memset(mean_cols[:], 0.0)
+        gain_cols = const.tile([P, BLOCK], F32, name="gain_cols", align_bytes=64)
+        nc.vector.memset(gain_cols[:], 0.0)
 
         w_words = w_sb[:].bitcast(F32).rearrange("o (m p u) -> o m u p", m=HALVES, u=2)
         w_turned = turn_psum.tile([P, HALVES, 2, P], F32, name="w_turned")
@@ -228,37 +230,51 @@ def tile_nonlocalblocknd_pc_t_kernel(tc, y, w_w, w_b, bn_gamma, out_0, out_1, ou
                             out=wy_rows[b, m, :, sfirst:done], in_=wy_of[(b, m)][:, sfirst:done]
                         )
 
+        last = len(squares) - 1
         sums = const.tile([P, HALVES], F32, name="sums")
         nc.vector.tensor_reduce(out=sums[:], in_=stats[:, 0], axis=mybir.AxisListType.X, op=ALU.add)
+        early = const.tile([P, HALVES], F32, name="early")
+        nc.vector.tensor_reduce(out=early[:], in_=stats[:, 1, :, 0:last], axis=mybir.AxisListType.X, op=ALU.add)
         off = const.tile([P, HALVES], F32, name="off")
         nc.vector.scalar_tensor_tensor(
             out=off[:], in0=sums[:], scalar=1.0 / COUNT, in1=neg_shift[:], op0=ALU.mult, op1=ALU.add
         )
-        off2 = const.tile([P, HALVES], F32, name="off2")
-        nc.vector.tensor_tensor(out=off2[:], in0=off[:], in1=off[:], op=ALU.mult)
+        early_eps = const.tile([P, HALVES], F32, name="early_eps")
         nc.vector.tensor_scalar(
-            out=res_cols[:, 0:HALVES], in0=sums[:], scalar1=1.0 / COUNT, scalar2=None, op0=ALU.mult
+            out=early_eps[:], in0=early[:], scalar1=1.0 / COUNT, scalar2=BN_EPS, op0=ALU.mult, op1=ALU.add
         )
-        last = len(squares) - 1
-        early = const.tile([P, HALVES], F32, name="early")
-        nc.vector.tensor_reduce(out=early[:], in_=stats[:, 1, :, 0:last], axis=mybir.AxisListType.X, op=ALU.add)
-        rest = const.tile([P, HALVES], F32, name="rest")
-        nc.vector.scalar_tensor_tensor(
-            out=rest[:], in0=early[:], scalar=1.0 / COUNT, in1=off2[:], op0=ALU.mult, op1=ALU.subtract
-        )
-        var = const.tile([P, HALVES], F32, name="var")
-        nc.vector.scalar_tensor_tensor(
-            out=var[:], in0=stats[:, 1, :, last], scalar=1.0 / COUNT, in1=rest[:], op0=ALU.mult, op1=ALU.add
-        )
-        inv_std = const.tile([P, HALVES], F32, name="inv_std")
-        nc.scalar.activation(out=inv_std[:], in_=var[:], func=ACT.Abs_reciprocal_sqrt, bias=BN_EPS)
-        nc.vector.tensor_tensor(
-            out=res_cols[:, HALVES : 2 * HALVES], in0=inv_std[:], in1=per_channel[:, HALVES : 2 * HALVES], op=ALU.mult
-        )
-        res_blocks = const.tile([P, BLOCK], F32, name="res_blocks", align_bytes=64)
-        nc.vector.transpose(out=res_blocks[:], in_=res_cols[:])
-        mean_rows = out_1.rearrange("(m q i) -> m q i", m=HALVES, i=BLOCK)
-        gain_rows = out_2.rearrange("(m q i) -> m q i", m=HALVES, i=BLOCK)
+        neg_rest = const.tile([P, HALVES], F32, name="neg_rest")
         for m in range(HALVES):
-            nc.sync.dma_start(out=gain_rows[m], in_=res_blocks[HALVES + m : P : BLOCK, :])
-            nc.scalar.dma_start(out=mean_rows[m], in_=res_blocks[m:P:BLOCK, :])
+            nc.vector.scalar_tensor_tensor(
+                out=neg_rest[:, m : m + 1],
+                in0=off[:, m : m + 1],
+                scalar=off[:, m : m + 1],
+                in1=early_eps[:, m : m + 1],
+                op0=ALU.mult,
+                op1=ALU.subtract,
+            )
+        nc.vector.tensor_scalar(
+            out=mean_cols[:, 0:HALVES], in0=sums[:], scalar1=1.0 / COUNT, scalar2=None, op0=ALU.mult
+        )
+        mean_blocks = const.tile([P, BLOCK], F32, name="mean_blocks", align_bytes=64)
+        nc.vector.transpose(out=mean_blocks[:], in_=mean_cols[:])
+        mean_rows = out_1.rearrange("(m q i) -> m q i", m=HALVES, i=BLOCK)
+        for m in range(HALVES):
+            nc.sync.dma_start(out=mean_rows[m], in_=mean_blocks[m:P:BLOCK, :])
+        inv_std = const.tile([P, HALVES], F32, name="inv_std")
+        for m in range(HALVES):
+            nc.scalar.activation(
+                out=inv_std[:, m : m + 1],
+                in_=stats[:, 1, m, last : last + 1],
+                func=ACT.Abs_reciprocal_sqrt,
+                scale=-1.0 / COUNT,
+                bias=neg_rest[:, m : m + 1],
+            )
+        nc.vector.tensor_tensor(
+            out=gain_cols[:, 0:HALVES], in0=inv_std[:], in1=per_channel[:, HALVES : 2 * HALVES], op=ALU.mult
+        )
+        gain_blocks = const.tile([P, BLOCK], F32, name="gain_blocks", align_bytes=64)
+        nc.vector.transpose(out=gain_blocks[:], in_=gain_cols[:])
+        gain_rows = out_2.rearrange("(m q i) -> m q i", m=HALVES, i=BLOCK)
+        nc.sync.dma_start(out=gain_rows[0], in_=gain_blocks[0:P:BLOCK, :])
+        nc.scalar.dma_start(out=gain_rows[1], in_=gain_blocks[1:P:BLOCK, :])

@@ -27,7 +27,7 @@ BLOCK = 32
 LOAD_WIDTHS = ((512, 512, 512, 512), (1024, 1024), (2048,), (2048,))
 UNIT_WIDTHS = ((512,) * 4,) * 4
 SQUARE_WIDTHS = ((512, 512, 1024), (2048,), (1536, 512), (512,) * 4)
-STORE_WIDTHS = ((1024, 1024),) * 4
+STORE_WIDTHS = ((1024, 1024),) * 3 + ((1024, 512, 512),)
 VECTOR_BANKS = 10
 
 FLOPS = 2 * BATCH * C_OUT * D_IN * POINTS

@@ -19,7 +19,7 @@ C_OUT = 256
 HALVES = C_OUT // P
 POINTS = 8 * 16 * 16
 BANK = 512
-RUN = 4
+RUN = 8
 COUNT = BATCH * POINTS
 BN_EPS = 1e-5
 BLOCK = 32

from contextlib import ExitStack

import concourse.mybir as mybir
from concourse.masks import make_identity

F32 = mybir.dt.float32
BF16 = mybir.dt.bfloat16
U32 = mybir.dt.uint32
U8 = mybir.dt.uint8
FP8X4 = mybir.dt.float8_e4m3fn_x4
ACT = mybir.ActivationFunctionType
ALU = mybir.AluOpType

P = 128
PACK = 4
BATCH = 4
D_IN = P * PACK
C_OUT = 256
HALVES = C_OUT // P
POINTS = 8 * 16 * 16
BANK = 512
RUN = 8
COUNT = BATCH * POINTS
BN_EPS = 1e-5
BLOCK = 32

LOAD_WIDTHS = ((512, 512, 512, 512), (1024, 1024), (2048,), (2048,))
UNIT_WIDTHS = ((512,) * 4,) * 4
SQUARE_WIDTHS = ((512, 512, 1024), (2048,), (1536, 512), (512,) * 4)
STORE_WIDTHS = ((1024, 1024),) * 3 + ((1024, 512, 512),)
VECTOR_BANKS = 10

FLOPS = 2 * BATCH * C_OUT * D_IN * POINTS


def cut(widths_by_batch):
    pieces = []
    for b in range(BATCH):
        first = 0
        for width in widths_by_batch[b]:
            pieces.append((b, first, width))
            first += width
        assert first == POINTS
    return pieces


def tile_nonlocalblocknd_pc_t_kernel(tc, y, w_w, w_b, bn_gamma, out_0, out_1, out_2):
    nc = tc.nc
    loads = cut(LOAD_WIDTHS)
    units = cut(UNIT_WIDTHS)
    squares = cut(SQUARE_WIDTHS)
    stores = cut(STORE_WIDTHS)
    passes = []
    for u, (b, first, width) in enumerate(units):
        for c in range(0, width, BANK):
            passes.append((u, b, first + c, min(BANK, width), c))
    slots = max(len(passes), len(squares))

    with ExitStack() as ctx:
        const = ctx.enter_context(tc.tile_pool(name="const", bufs=1))
        y_pool = ctx.enter_context(tc.tile_pool(name="y_in", bufs=1))
        grouped_pool = ctx.enter_context(tc.tile_pool(name="grouped", bufs=3))
        mx_pool = ctx.enter_context(tc.tile_pool(name="mx", bufs=1))
        wy_pool = ctx.enter_context(tc.tile_pool(name="wy", bufs=BATCH * HALVES))
        squared_pool = ctx.enter_context(tc.tile_pool(name="squared", bufs=2))
        turn_psum = ctx.enter_context(tc.psum_pool(name="turn", bufs=1))
        acc_psum = ctx.enter_context(tc.psum_pool(name="acc", bufs=6))
        ctx.enter_context(tc.manual_schedule())

        w_sb = const.tile([P, HALVES * D_IN], BF16, name="w_sb")
        nc.sync.dma_start(
            out=w_sb[:].rearrange("o (m d) -> o m d", m=HALVES),
            in_=w_w.rearrange("(m o) d -> o m d", o=P),
        )
        y_rows = y.rearrange("b (p t) f h w -> b p t (f h w)", t=PACK)
        y_piece = {}
        for b, first, width in loads:
            piece = y_pool.tile([P, PACK, width], BF16, name="y_%d_%d" % (b, first))
            nc.sync.dma_start(out=piece[:], in_=y_rows[b, :, :, first : first + width])
            y_piece[(b, first)] = piece

        def y_view(b, first, width):
            for lb, lfirst, lwidth in loads:
                if lb == b and lfirst <= first and first + width <= lfirst + lwidth:
                    return y_piece[(lb, lfirst)][:, :, first - lfirst : first - lfirst + width]
            raise ValueError("a unit must lie inside one load")

        vec_rows = const.tile([2 * HALVES, P], BF16, name="vec_rows")
        nc.scalar.dma_start(out=vec_rows[0:HALVES, :], in_=w_b.rearrange("(r c) -> r c", c=P))
        nc.scalar.dma_start(
            out=vec_rows[HALVES : 2 * HALVES, :], in_=bn_gamma.rearrange("(r c) -> r c", c=P)
        )

        ident = const.tile([P, P], F32, name="ident")
        make_identity(nc, ident[:])
        one = const.tile([P, 1], F32, name="one")
        nc.vector.memset(one[:], 1.0)
        warm = const.tile([P, 1], F32, name="warm")
        nc.scalar.activation(out=warm[:], in_=one[:], func=ACT.Abs_reciprocal_sqrt)
        stats = const.tile([P, 2, HALVES, slots], F32, name="stats")
        nc.vector.memset(stats[:], 0.0)
        vec_sq = const.tile([P, P], F32, name="vec_sq")
        nc.vector.memset(vec_sq[:], 0.0)
        mean_cols = const.tile([P, BLOCK], F32, name="mean_cols", align_bytes=64)
        nc.vector.memset(mean_cols[:], 0.0)
        gain_cols = const.tile([P, BLOCK], F32, name="gain_cols", align_bytes=64)
        nc.vector.memset(gain_cols[:], 0.0)

        w_words = w_sb[:].bitcast(F32).rearrange("o (m p u) -> o m u p", m=HALVES, u=2)
        w_turned = turn_psum.tile([P, HALVES, 2, P], F32, name="w_turned")
        for m in range(HALVES):
            for u in range(2):
                nc.tensor.transpose(out=w_turned[:, m, u, :], in_=w_words[:, m, u, :], identity=ident[:])
        w_grouped = const.tile([P, C_OUT * PACK], BF16, name="w_grouped", align_bytes=64)
        nc.scalar.copy(
            out=w_grouped[:].bitcast(F32).rearrange("p (m o u) -> p m o u", m=HALVES, u=2),
            in_=w_turned[:].rearrange("p m u o -> p m o u"),
        )
        w_codes = const.tile([P, C_OUT], U32, name="w_codes", align_bytes=64)
        w_scales = const.tile([P, C_OUT], U8, name="w_scales", align_bytes=64)

        nc.scalar.copy(out=vec_sq[0 : 2 * HALVES, :], in_=vec_rows[:])
        vec_turned = turn_psum.tile([P, P], F32, name="vec_turned")
        nc.tensor.transpose(out=vec_turned[:], in_=vec_sq[:], identity=ident[:])
        per_channel = const.tile([P, 2 * HALVES], F32, name="per_channel")
        nc.scalar.copy(out=per_channel[:], in_=vec_turned[:, 0 : 2 * HALVES])

        wy_rows = out_0.rearrange("b (m o) f h w -> b m o (f h w)", o=P)
        grouped_of = {}
        codes_of = {}
        scales_of = {}
        acc_of = {}
        wy_of = {}
        neg_shift = const.tile([P, HALVES], F32, name="neg_shift")

        def regroup(u):
            b, first, width = units[u]
            grouped = grouped_pool.tile([P, width, PACK], BF16, name="grouped", align_bytes=64)
            nc.vector.tensor_copy(
                out=grouped[:].rearrange("p (c i) t -> p c t i", i=RUN),
                in_=y_view(b, first, width).rearrange("p t (c i) -> p c t i", i=RUN),
            )
            grouped_of[u] = grouped

        def quantise(u):
            width = units[u][2]
            codes = mx_pool.tile([P, width], U32, name="y_codes_%d" % u, align_bytes=64)
            scales = mx_pool.tile([P, width], U8, name="y_scales_%d" % u, align_bytes=64)
            nc.vector.quantize_mx(
                out=codes[:].bitcast(FP8X4),
                scales=scales[:],
                in_=grouped_of[u][:].rearrange("p n t -> p (n t)"),
            )
            codes_of[u] = codes
            scales_of[u] = scales

        def multiply(i):
            u, b, first, width, c = passes[i]
            for m in range(HALVES):
                acc = acc_psum.tile([P, width], F32, name="acc")
                nc.tensor.matmul_mx(
                    out=acc[:],
                    lhsT=w_codes[:, m * P : (m + 1) * P].bitcast(FP8X4),
                    lhsT_scale=w_scales[:, m * P : (m + 1) * P],
                    rhs=codes_of[u][:, c : c + width].bitcast(FP8X4),
                    rhs_scale=scales_of[u][:, c : c + width],
                    start=True,
                    stop=True,
                )
                acc_of[(i, m)] = acc

        def add_bias(i, m):
            u, b, first, width, c = passes[i]
            if first == 0:
                wy_of[(b, m)] = wy_pool.tile([P, POINTS], F32, name="wy")
            if HALVES * i + m >= HALVES * len(passes) - VECTOR_BANKS:
                nc.vector.tensor_scalar(
                    out=wy_of[(b, m)][:, first : first + width],
                    in0=acc_of[(i, m)][:],
                    scalar1=per_channel[:, m : m + 1],
                    scalar2=None,
                    op0=ALU.add,
                    op1=ALU.add,
                    accum_out=stats[:, 0, m, i : i + 1],
                )
            else:
                nc.scalar.activation(
                    out=wy_of[(b, m)][:, first : first + width],
                    in_=acc_of[(i, m)][:],
                    func=ACT.Identity,
                    bias=per_channel[:, m : m + 1],
                    accum_out=stats[:, 0, m, i : i + 1],
                )

        def square(g, m):
            b, first, width = squares[g]
            squared = squared_pool.tile([P, width], BF16, name="squared")
            nc.scalar.activation(
                out=squared[:],
                in_=wy_of[(b, m)][:, first : first + width],
                func=ACT.Square,
                bias=neg_shift[:, m : m + 1],
                accum_out=stats[:, 1, m, g : g + 1],
            )

        regroup(0)
        nc.vector.quantize_mx(out=w_codes[:].bitcast(FP8X4), scales=w_scales[:], in_=w_grouped[:])
        quantise(0)
        regroup(1)
        for u in range(1, len(units)):
            if u + 1 < len(units):
                regroup(u + 1)
            quantise(u)

        for i, (u, b, first, width, c) in enumerate(passes):
            done = first + width
            multiply(i)
            for m in range(HALVES):
                add_bias(i, m)
            if i == 0:
                nc.scalar.mul(out=neg_shift[:], in_=stats[:, 0, :, 0], mul=-1.0 / width)
            for g, (gb, gfirst, gwidth) in enumerate(squares):
                if gb == b and gfirst + gwidth == done:
                    for m in range(HALVES):
                        square(g, m)
            for sb, sfirst, swidth in stores:
                if sb == b and sfirst + swidth == done:
                    for m in range(HALVES):
                        nc.sync.dma_start(
                            out=wy_rows[b, m, :, sfirst:done], in_=wy_of[(b, m)][:, sfirst:done]
                        )

        last = len(squares) - 1
        sums = const.tile([P, HALVES], F32, name="sums")
        nc.vector.tensor_reduce(out=sums[:], in_=stats[:, 0], axis=mybir.AxisListType.X, op=ALU.add)
        early = const.tile([P, HALVES], F32, name="early")
        nc.vector.tensor_reduce(out=early[:], in_=stats[:, 1, :, 0:last], axis=mybir.AxisListType.X, op=ALU.add)
        off = const.tile([P, HALVES], F32, name="off")
        nc.vector.scalar_tensor_tensor(
            out=off[:], in0=sums[:], scalar=1.0 / COUNT, in1=neg_shift[:], op0=ALU.mult, op1=ALU.add
        )
        early_eps = const.tile([P, HALVES], F32, name="early_eps")
        nc.vector.tensor_scalar(
            out=early_eps[:], in0=early[:], scalar1=1.0 / COUNT, scalar2=BN_EPS, op0=ALU.mult, op1=ALU.add
        )
        neg_rest = const.tile([P, HALVES], F32, name="neg_rest")
        for m in range(HALVES):
            nc.vector.scalar_tensor_tensor(
                out=neg_rest[:, m : m + 1],
                in0=off[:, m : m + 1],
                scalar=off[:, m : m + 1],
                in1=early_eps[:, m : m + 1],
                op0=ALU.mult,
                op1=ALU.subtract,
            )
        nc.vector.tensor_scalar(
            out=mean_cols[:, 0:HALVES], in0=sums[:], scalar1=1.0 / COUNT, scalar2=None, op0=ALU.mult
        )
        mean_blocks = const.tile([P, BLOCK], F32, name="mean_blocks", align_bytes=64)
        nc.vector.transpose(out=mean_blocks[:], in_=mean_cols[:])
        mean_rows = out_1.rearrange("(m q i) -> m q i", m=HALVES, i=BLOCK)
        for m in range(HALVES):
            nc.sync.dma_start(out=mean_rows[m], in_=mean_blocks[m:P:BLOCK, :])
        inv_std = const.tile([P, HALVES], F32, name="inv_std")
        for m in range(HALVES):
            nc.scalar.activation(
                out=inv_std[:, m : m + 1],
                in_=stats[:, 1, m, last : last + 1],
                func=ACT.Abs_reciprocal_sqrt,
                scale=-1.0 / COUNT,
                bias=neg_rest[:, m : m + 1],
            )
        nc.vector.tensor_tensor(
            out=gain_cols[:, 0:HALVES], in0=inv_std[:], in1=per_channel[:, HALVES : 2 * HALVES], op=ALU.mult
        )
        gain_blocks = const.tile([P, BLOCK], F32, name="gain_blocks", align_bytes=64)
        nc.vector.transpose(out=gain_blocks[:], in_=gain_cols[:])
        gain_rows = out_2.rearrange("(m q i) -> m q i", m=HALVES, i=BLOCK)
        nc.sync.dma_start(out=gain_rows[0], in_=gain_blocks[0:P:BLOCK, :])
        nc.scalar.dma_start(out=gain_rows[1], in_=gain_blocks[1:P:BLOCK, :])
